import numpy as np
import ml_dtypes


def mxq(x, axis, fmt="e4m3"):
    dtype, down = {"e4m3": (ml_dtypes.float8_e4m3fn, 7), "e5m2": (ml_dtypes.float8_e5m2, 14)}[fmt]
    v = np.moveaxis(np.asarray(x, np.float32).astype(ml_dtypes.bfloat16).astype(np.float64), axis, -1)
    blocks = v.reshape(v.shape[:-1] + (-1, 32))
    amax = np.abs(blocks).max(-1, keepdims=True)
    byte = np.maximum(np.where(amax > 0, np.frexp(amax)[1] - 1 + 127, 0) - down, 1)
    scale = np.exp2(byte - 127.0)
    codes = (blocks / scale).astype(np.float32).astype(dtype).astype(np.float64)
    return np.moveaxis((codes * scale).reshape(v.shape), -1, axis)


WIDE = False


def mx_kscale(k):
    if not WIDE:
        return np.ones(k)
    levels = np.array([10, -10, 5, -5, 0])
    a = np.random.permutation(np.resize(levels, k // 512 * 4)).reshape(k // 512, 4)
    idx = np.arange(k)
    return np.exp2(a[idx // 512, idx % 128 // 32])


BF16 = ml_dtypes.bfloat16


def bf(x):
    return np.asarray(x, np.float32).astype(BF16)


def f64(x):
    return np.asarray(x).astype(np.float64)


E2M1 = np.array([0.0, 0.5, 1.0, 1.5, 2.0, 3.0, 4.0, 6.0, -0.0, -0.5, -1.0, -1.5, -2.0, -3.0, -4.0, -6.0])


def pack_weight(w, fmt):
    k, n = w.shape
    w = f64(bf(w)).reshape(k // 32, 32, n)
    amax = np.abs(w).max(1)
    if fmt == "e4m3":
        byte = np.frexp(amax)[1] - 1 + 127 - 7
    else:
        mant, ex = np.frexp(amax / 6.0)
        byte = np.where(mant > 0.5, ex, ex - 1) + 127
    byte = np.clip(np.where(amax > 0, byte, 1), 1, 254)
    scaled = (w * np.exp2(127.0 - byte)[:, None, :]).reshape(k, n).astype(np.float32)
    by_word = np.ascontiguousarray(scaled.reshape(k // 512, 128, 4, n).transpose(0, 1, 3, 2))
    if fmt == "e4m3":
        words = by_word.astype(ml_dtypes.float8_e4m3fn).view(np.uint8)
    else:
        c = by_word.astype(ml_dtypes.float4_e2m1fn).view(np.uint8) & 0xF
        words = c[..., 0::2] | (c[..., 1::2] << 4)
    return np.ascontiguousarray(words), np.ascontiguousarray(byte.astype(np.uint8).reshape(k // 512, 16, n))


def unpack_weight(words, scales, fmt):
    g, p, n, _ = words.shape
    if fmt == "e4m3":
        vals = np.ascontiguousarray(words).view(ml_dtypes.float8_e4m3fn).astype(np.float64)
    else:
        nib = np.empty((g, p, n, 4), np.uint8)
        nib[..., 0::2] = words & 0xF
        nib[..., 1::2] = words >> 4
        vals = E2M1[nib]
    vals = vals * np.repeat(np.exp2(scales.astype(np.float64) - 127.0), 8, axis=1)[..., None]
    return vals.transpose(0, 1, 3, 2).reshape(g * 512, n)


B, D = 128, 192


def setup_inputs():
    a = mx_kscale(D * D)[::D]
    c = np.concatenate((a, np.ones(D)))
    hspatial = bf(np.random.standard_normal((B, D)) * a)
    htext = bf(np.random.standard_normal((B, D)))
    W_L = bf(np.random.standard_normal((2 * D, 2 * D)) / np.sqrt(2 * D) / c)
    b_L = bf(np.random.standard_normal(2 * D) * 0.3)
    w2 = np.random.standard_normal((2 * D, D * D)) / D / np.repeat(a, D)
    words, scales = pack_weight(np.ascontiguousarray(w2.T), "e4m3")
    b_L2 = bf(np.random.standard_normal(2 * D) * 0.3)
    return {"hspatial": hspatial,
            "htext": htext,
            "W_L": W_L,
            "b_L": b_L,
            "W_L2_words": words,
            "W_L2_scales": scales,
            "b_L2": b_L2}


def reference(hspatial, htext, W_L, b_L, W_L2_words, W_L2_scales, b_L2):
    hs, ht = f64(hspatial), f64(htext)
    g = np.concatenate((hs, ht), axis=1) @ f64(W_L).T + f64(b_L)
    v = (hs[:, :, None] * ht[:, None, :]).reshape(hs.shape[0], -1)
    u = (mxq(v, 1, "e4m3") @ unpack_weight(W_L2_words, W_L2_scales, "e4m3")) + f64(b_L2)
    return np.concatenate((g, u), axis=1)

@@ -1,0 +1,226 @@
+from contextlib import ExitStack
+
+import concourse.bass as bass
+import concourse.mybir as mybir
+import concourse.tile as tile
+from concourse.masks import make_identity
+
+BF16 = mybir.dt.bfloat16
+F32 = mybir.dt.float32
+I32 = mybir.dt.int32
+U8 = mybir.dt.uint8
+U32 = mybir.dt.uint32
+FP8X4 = mybir.dt.float8_e4m3fn_x4
+MULT = mybir.AluOpType.mult
+ADD = mybir.AluOpType.add
+
+P = 128
+B = 128
+D = 192
+N = 2 * D
+GROUPS = D * D // 512
+WPI = D // 4
+PERIOD = 3
+GPB = 4
+BANKS = GROUPS // GPB
+LEAD = 4
+
+FLOPS = 2 * B * D * D * N + 2 * B * N * N
+
+
+def tile_deepandwide_w_kernel(tc, hspatial, htext, W_L, b_L, W_L2_words, W_L2_scales, b_L2, out):
+    nc = tc.nc
+    with ExitStack() as ctx:
+        keep = ctx.enter_context(tc.tile_pool(name="keep", bufs=1))
+        ring = ctx.enter_context(tc.tile_pool(name="ring", bufs=3))
+        ps_acc = ctx.enter_context(tc.psum_pool(name="ps_acc", bufs=1))
+        ps_hs = ctx.enter_context(tc.psum_pool(name="ps_hs", bufs=3))
+        ps_tp = ctx.enter_context(tc.psum_pool(name="ps_tp", bufs=3))
+        ctx.enter_context(tc.manual_schedule())
+
+        x_sb = keep.tile([P, 2 * D], BF16, name="x_sb", align_bytes=64)
+        bt = keep.tile([P, P], BF16, name="bt")
+        planes = keep.tile([P, (GROUPS // 4) * N], U8, name="planes", align_bytes=64)
+        ident_b = keep.tile([P, P], BF16, name="ident_b")
+        ident_f = keep.tile([P, P], F32, name="ident_f")
+        wl_sb = keep.tile([P, 3, N], BF16, name="wl_sb")
+        w_tiles = [keep.tile([P, GPB, 4 * N], U8, name="w%d" % n, align_bytes=64) for n in range(BANKS)]
+        vw = [keep.tile([P, GPB * B], U32, name="vw%d" % n, align_bytes=64) for n in range(BANKS)]
+        vpl = [keep.tile([P, GPB * B], U8, name="vpl%d" % n, align_bytes=64) for n in range(BANKS)]
+        sel = [keep.tile([P, 32, WPI], BF16, name="sel%d" % s) for s in range(4)]
+
+        nc.vector.memset(bt[:], 0.0)
+        nc.vector.memset(planes[:].bitcast(I32), 0)
+        make_identity(nc, ident_b[:])
+        make_identity(nc, ident_f[:])
+
+        nc.sync.dma_start(out=x_sb[:, 0:D], in_=hspatial)
+        nc.sync.dma_start(out=x_sb[:, D : 2 * D], in_=htext)
+        nc.scalar.dma_start(out=bt[0:3, :], in_=b_L.rearrange("(a n) -> a n", a=3))
+        nc.scalar.dma_start(out=bt[3:6, :], in_=b_L2.rearrange("(a n) -> a n", a=3))
+        sc_view = W_L2_scales.bitcast(I32).rearrange("(col a) q w -> q a col w", a=4)
+        for quad in range(4):
+            for r in range(4):
+                nc.sync.dma_start(
+                    out=planes[32 * quad + r : 32 * quad + 16 : 4, :]
+                    .bitcast(I32)
+                    .rearrange("a (col w) -> a col w", w=N // 4),
+                    in_=sc_view[4 * quad + r],
+                )
+        w_view = (
+            W_L2_words.rearrange("g p n t -> g p (n t)")
+            .bitcast(I32)
+            .rearrange("(G c) p w -> c p G w", c=PERIOD)
+        )
+        for n in range(BANKS):
+            sup, c = divmod(n, PERIOD)
+            src = w_view[c]
+            dst = w_tiles[n][:].bitcast(I32)
+            cuts = [(0, 4)] if n < BANKS - 1 else [(0, 2), (2, 3), (3, 4)]
+            for lo, hi in cuts:
+                nc.sync.dma_start(out=dst[:, lo:hi, :], in_=src[:, GPB * sup + lo : GPB * sup + hi, :])
+            if n == 1:
+                nc.sync.dma_start(out=wl_sb[:], in_=W_L.rearrange("(a p) k -> p a k", p=P))
+
+        def build_sel(s):
+            nc.scalar.copy(
+                out=sel[s][:],
+                in_=ident_b[:, 32 * s : 32 * s + 32].unsqueeze(2).to_broadcast([P, 32, WPI]),
+            )
+
+        build_sel(0)
+
+        ps_x = ps_tp.tile([P, 3, P], BF16, name="ps_x", tag="tp")
+        for j in range(3):
+            nc.tensor.transpose(ps_x[:, j, :], x_sb[:, P * j : P * j + P], ident_b[:])
+        xT = keep.tile([P, 3, P], BF16, name="xT")
+        nc.scalar.copy(out=xT[:], in_=ps_x[:])
+
+        htx = keep.tile([P, 2, 8, WPI], F32, name="htx")
+        nc.vector.tensor_copy(
+            out=htx[:],
+            in_=x_sb[:, D : 2 * D]
+            .bitcast(F32)
+            .rearrange("p (r u) -> p u r", u=2)
+            .unsqueeze(2)
+            .to_broadcast([P, 2, 8, WPI]),
+        )
+        htx_flat = htx[:].rearrange("p u a r -> p u (a r)")
+        ht = []
+        for c in range(PERIOD):
+            pht = ps_tp.tile([P, 2, P], F32, name="pht%d" % c, tag="tp")
+            for u in range(2):
+                nc.tensor.transpose(pht[:, u, :], htx_flat[:, u, P * c : P * c + P], ident_f[:])
+            ht_c = keep.tile([P, B, 2, 2], BF16, name="ht%d" % c)
+            nc.vector.tensor_copy(
+                out=ht_c[:].rearrange("p b u e -> p (b u e)").bitcast(F32).rearrange("p (b u) -> p b u", u=2),
+                in_=pht[:].rearrange("p u b -> p b u"),
+            )
+            ht.append(ht_c)
+
+        acc_a = ps_acc.tile([P, 256], F32, name="acc_a")
+        acc_b = ps_acc.tile([P, 128], F32, name="acc_b")
+
+        hs2_of = {}
+        vin_of = {}
+
+        def group_of(n, gi):
+            sup, c = divmod(n, PERIOD)
+            return PERIOD * (GPB * sup + gi) + c
+
+        def spread(n):
+            hs_ps = ps_hs.tile([P, GPB, B], F32, name="hs_ps", tag="hs")
+            for gi in range(GPB):
+                g = group_of(n, gi)
+                half, gl = divmod(g, 48)
+                s, blk = divmod(gl, 12)
+                nc.tensor.matmul(
+                    hs_ps[:, gi, :],
+                    lhsT=sel[s][:].rearrange("p i r -> p (i r)")[:, P * blk : P * blk + P],
+                    rhs=xT[:, half, :],
+                    start=True,
+                    stop=True,
+                )
+            hs2 = ring.tile([P, GPB, B, 2], BF16, name="hs2", tag="hs2")
+            nc.scalar.copy(out=hs2[:], in_=hs_ps[:].unsqueeze(3).to_broadcast([P, GPB, B, 2]))
+            hs2_of[n] = hs2
+
+        def product(n):
+            c = n % PERIOD
+            vin = ring.tile([P, GPB, B, 2, 2], BF16, name="vin", tag="vin", align_bytes=64)
+            nc.vector.tensor_tensor(
+                out=vin[:],
+                in0=ht[c][:].unsqueeze(1).to_broadcast([P, GPB, B, 2, 2]),
+                in1=hs2_of[n][:].unsqueeze(3).to_broadcast([P, GPB, B, 2, 2]),
+                op=MULT,
+            )
+            vin_of[n] = vin
+
+        def quantise(n):
+            nc.vector.quantize_mx(
+                out=vw[n][:].bitcast(FP8X4),
+                scales=vpl[n][:],
+                in_=vin_of[n][:].rearrange("p g b u e -> p (g b u e)"),
+            )
+
+        def passes(n):
+            for gi in range(GPB):
+                g = group_of(n, gi)
+                col, a = divmod(g, 4)
+                first = n == 0 and gi == 0
+                last = n == BANKS - 1 and gi == GPB - 1
+                for acc, lo, hi in ((acc_a, 0, 256), (acc_b, 256, 384)):
+                    nc.tensor.matmul_mx(
+                        out=acc[:],
+                        lhsT=vw[n][:, B * gi : B * gi + B].bitcast(FP8X4),
+                        lhsT_scale=vpl[n][:, B * gi : B * gi + B],
+                        rhs=w_tiles[n][:, gi, 4 * lo : 4 * hi].bitcast(FP8X4),
+                        rhs_scale=planes[4 * a : P, N * col + lo : N * col + hi],
+                        start=first,
+                        stop=last,
+                    )
+
+        bias_bc = keep.tile([P, 2 * N], F32, name="bias_bc")
+
+        def deep():
+            ps_b = ps_tp.tile([P, P], BF16, name="ps_b", tag="tp")
+            nc.tensor.transpose(ps_b[:], bt[:], ident_b[:])
+            btT = keep.tile([P, P], BF16, name="btT")
+            nc.scalar.copy(out=btT[:], in_=ps_b[:])
+            ps_bb = ps_tp.tile([P, 6, P], BF16, name="ps_bb", tag="tp")
+            for m in range(6):
+                nc.tensor.transpose(ps_bb[:, m, :], btT[:, m : m + 1].to_broadcast([P, P]), ident_b[:])
+            nc.scalar.copy(out=bias_bc[:], in_=ps_bb[:].rearrange("p m n -> p (m n)"))
+            wlT = keep.tile([P, 3, N], BF16, name="wlT")
+            for j in range(3):
+                ps_w = ps_tp.tile([P, 3, P], BF16, name="ps_w", tag="tp")
+                for a in range(3):
+                    nc.tensor.transpose(ps_w[:, a, :], wl_sb[:, a, P * j : P * j + P], ident_b[:])
+                nc.scalar.copy(out=wlT[:, j, :], in_=ps_w[:].rearrange("p a n -> p (a n)"))
+            acc_g = ps_tp.tile([P, N], F32, name="acc_g", tag="tp")
+            for j in range(3):
+                nc.tensor.matmul(acc_g[:], lhsT=xT[:, j, :], rhs=wlT[:, j, :], start=(j == 0), stop=(j == 2))
+            return acc_g
+
+        for step in range(BANKS + LEAD):
+            if step < BANKS:
+                spread(step)
+                if step % 3 == 0 and step // 3 + 1 < 4:
+                    build_sel(step // 3 + 1)
+            if 0 <= step - 1 < BANKS:
+                product(step - 1)
+            if 0 <= step - 2 < BANKS:
+                quantise(step - 2)
+            if 0 <= step - LEAD < BANKS:
+                passes(step - LEAD)
+            if step == 8:
+                acc_g = deep()
+            if step == BANKS + 2:
+                g_sb = keep.tile([P, N], F32, name="g_sb")
+                nc.vector.tensor_tensor(out=g_sb[:], in0=acc_g[:], in1=bias_bc[:, 0:N], op=ADD)
+                nc.sync.dma_start(out=out[:, 0:N], in_=g_sb[:])
+
+        u_sb = keep.tile([P, N], F32, name="u_sb")
+        nc.vector.tensor_tensor(out=u_sb[:, 0:256], in0=acc_a[:], in1=bias_bc[:, N : N + 256], op=ADD)
+        nc.vector.tensor_tensor(out=u_sb[:, 256:N], in0=acc_b[:], in1=bias_bc[:, N + 256 : 2 * N], op=ADD)
+        nc.sync.dma_start(out=out[:, N : 2 * N], in_=u_sb[:])

@@ -23,7 +23,7 @@ WPI = D // 4
 PERIOD = 3
 GPB = 4
 BANKS = GROUPS // GPB
-LEAD = 4
+LEAD = 3
 
 FLOPS = 2 * B * D * D * N + 2 * B * N * N
 
@@ -34,8 +34,8 @@ def tile_deepandwide_w_kernel(tc, hspatial, htext, W_L, b_L, W_L2_words, W_L2_sc
         keep = ctx.enter_context(tc.tile_pool(name="keep", bufs=1))
         ring = ctx.enter_context(tc.tile_pool(name="ring", bufs=3))
         ps_acc = ctx.enter_context(tc.psum_pool(name="ps_acc", bufs=1))
-        ps_hs = ctx.enter_context(tc.psum_pool(name="ps_hs", bufs=3))
-        ps_tp = ctx.enter_context(tc.psum_pool(name="ps_tp", bufs=3))
+        ps_hs = ctx.enter_context(tc.psum_pool(name="ps_hs", bufs=4))
+        ps_tp = ctx.enter_context(tc.psum_pool(name="ps_tp", bufs=2))
         ctx.enter_context(tc.manual_schedule())
 
         x_sb = keep.tile([P, 2 * D], BF16, name="x_sb", align_bytes=64)
@@ -47,12 +47,12 @@ def tile_deepandwide_w_kernel(tc, hspatial, htext, W_L, b_L, W_L2_words, W_L2_sc
         w_tiles = [keep.tile([P, GPB, 4 * N], U8, name="w%d" % n, align_bytes=64) for n in range(BANKS)]
         vw = [keep.tile([P, GPB * B], U32, name="vw%d" % n, align_bytes=64) for n in range(BANKS)]
         vpl = [keep.tile([P, GPB * B], U8, name="vpl%d" % n, align_bytes=64) for n in range(BANKS)]
-        sel = [keep.tile([P, 32, WPI], BF16, name="sel%d" % s) for s in range(4)]
+        hrep = [keep.tile([P, 32, WPI], F32, name="hrep%d" % s) for s in range(6)]
 
         nc.vector.memset(bt[:], 0.0)
         nc.vector.memset(planes[:].bitcast(I32), 0)
-        make_identity(nc, ident_b[:])
         make_identity(nc, ident_f[:])
+        make_identity(nc, ident_b[:])
 
         nc.sync.dma_start(out=x_sb[:, 0:D], in_=hspatial)
         nc.sync.dma_start(out=x_sb[:, D : 2 * D], in_=htext)
@@ -82,19 +82,17 @@ def tile_deepandwide_w_kernel(tc, hspatial, htext, W_L, b_L, W_L2_words, W_L2_sc
             if n == 1:
                 nc.sync.dma_start(out=wl_sb[:], in_=W_L.rearrange("(a p) k -> p a k", p=P))
 
-        def build_sel(s):
-            nc.scalar.copy(
-                out=sel[s][:],
-                in_=ident_b[:, 32 * s : 32 * s + 32].unsqueeze(2).to_broadcast([P, 32, WPI]),
+        hsp = keep.tile([P, D, 2], BF16, name="hsp")
+        nc.vector.tensor_copy(out=hsp[:], in_=x_sb[:, 0:D].unsqueeze(2).to_broadcast([P, D, 2]))
+        hsp_w = hsp[:].rearrange("p i e -> p (i e)").bitcast(F32)
+
+        def build_hrep(eng_copy, s, lo, hi):
+            eng_copy(
+                out=hrep[s][:, lo:hi, :],
+                in_=hsp_w[:, 32 * s + lo : 32 * s + hi].unsqueeze(2).to_broadcast([P, hi - lo, WPI]),
             )
 
-        build_sel(0)
-
-        ps_x = ps_tp.tile([P, 3, P], BF16, name="ps_x", tag="tp")
-        for j in range(3):
-            nc.tensor.transpose(ps_x[:, j, :], x_sb[:, P * j : P * j + P], ident_b[:])
-        xT = keep.tile([P, 3, P], BF16, name="xT")
-        nc.scalar.copy(out=xT[:], in_=ps_x[:])
+        build_hrep(nc.scalar.copy, 0, 0, 16)
 
         htx = keep.tile([P, 2, 8, WPI], F32, name="htx")
         nc.vector.tensor_copy(
@@ -105,16 +103,25 @@ def tile_deepandwide_w_kernel(tc, hspatial, htext, W_L, b_L, W_L2_words, W_L2_sc
             .unsqueeze(2)
             .to_broadcast([P, 2, 8, WPI]),
         )
+        build_hrep(nc.vector.tensor_copy, 0, 16, 32)
+        for s in range(1, 6):
+            build_hrep(nc.scalar.copy, s, 0, 32)
         htx_flat = htx[:].rearrange("p u a r -> p u (a r)")
         ht = []
-        for c in range(PERIOD):
+
+        pht_of = {}
+
+        def turn_ht(c):
             pht = ps_tp.tile([P, 2, P], F32, name="pht%d" % c, tag="tp")
             for u in range(2):
                 nc.tensor.transpose(pht[:, u, :], htx_flat[:, u, P * c : P * c + P], ident_f[:])
+            pht_of[c] = pht
+
+        def keep_ht(c):
             ht_c = keep.tile([P, B, 2, 2], BF16, name="ht%d" % c)
             nc.vector.tensor_copy(
                 out=ht_c[:].rearrange("p b u e -> p (b u e)").bitcast(F32).rearrange("p (b u) -> p b u", u=2),
-                in_=pht[:].rearrange("p u b -> p b u"),
+                in_=pht_of[c][:].rearrange("p u b -> p b u"),
             )
             ht.append(ht_c)
 
@@ -129,21 +136,16 @@ def tile_deepandwide_w_kernel(tc, hspatial, htext, W_L, b_L, W_L2_words, W_L2_sc
             return PERIOD * (GPB * sup + gi) + c
 
         def spread(n):
+            sup, c = divmod(n, PERIOD)
             hs_ps = ps_hs.tile([P, GPB, B], F32, name="hs_ps", tag="hs")
             for gi in range(GPB):
-                g = group_of(n, gi)
-                half, gl = divmod(g, 48)
-                s, blk = divmod(gl, 12)
-                nc.tensor.matmul(
+                blk = PERIOD * gi + c
+                nc.tensor.transpose(
                     hs_ps[:, gi, :],
-                    lhsT=sel[s][:].rearrange("p i r -> p (i r)")[:, P * blk : P * blk + P],
-                    rhs=xT[:, half, :],
-                    start=True,
-                    stop=True,
+                    hrep[sup][:].rearrange("p i r -> p (i r)")[:, P * blk : P * blk + P],
+                    ident_f[:],
                 )
-            hs2 = ring.tile([P, GPB, B, 2], BF16, name="hs2", tag="hs2")
-            nc.scalar.copy(out=hs2[:], in_=hs_ps[:].unsqueeze(3).to_broadcast([P, GPB, B, 2]))
-            hs2_of[n] = hs2
+            hs2_of[n] = hs_ps
 
         def product(n):
             c = n % PERIOD
@@ -151,7 +153,12 @@ def tile_deepandwide_w_kernel(tc, hspatial, htext, W_L, b_L, W_L2_words, W_L2_sc
             nc.vector.tensor_tensor(
                 out=vin[:],
                 in0=ht[c][:].unsqueeze(1).to_broadcast([P, GPB, B, 2, 2]),
-                in1=hs2_of[n][:].unsqueeze(3).to_broadcast([P, GPB, B, 2, 2]),
+                in1=hs2_of[n][:]
+                .rearrange("p g b -> p (g b)")
+                .bitcast(BF16)
+                .rearrange("p (g b e) -> p g b e", g=GPB, e=2)
+                .unsqueeze(3)
+                .to_broadcast([P, GPB, B, 2, 2]),
                 op=MULT,
             )
             vin_of[n] = vin
@@ -182,42 +189,62 @@ def tile_deepandwide_w_kernel(tc, hspatial, htext, W_L, b_L, W_L2_words, W_L2_sc
 
         bias_bc = keep.tile([P, 2 * N], F32, name="bias_bc")
 
-        def deep():
-            ps_b = ps_tp.tile([P, P], BF16, name="ps_b", tag="tp")
-            nc.tensor.transpose(ps_b[:], bt[:], ident_b[:])
-            btT = keep.tile([P, P], BF16, name="btT")
-            nc.scalar.copy(out=btT[:], in_=ps_b[:])
+        xbT = keep.tile([P, 4, P], BF16, name="xbT")
+        wlT = keep.tile([P, 3, N], BF16, name="wlT")
+        late = {}
+
+        def deep_turn_x():
+            ps_x = ps_tp.tile([P, 4, P], BF16, name="ps_x", tag="tp")
+            for j in range(3):
+                nc.tensor.transpose(ps_x[:, j, :], x_sb[:, P * j : P * j + P], ident_b[:])
+            nc.tensor.transpose(ps_x[:, 3, :], bt[:], ident_b[:])
+            nc.scalar.copy(out=xbT[:], in_=ps_x[:])
+
+        def deep_spread_bias():
             ps_bb = ps_tp.tile([P, 6, P], BF16, name="ps_bb", tag="tp")
             for m in range(6):
-                nc.tensor.transpose(ps_bb[:, m, :], btT[:, m : m + 1].to_broadcast([P, P]), ident_b[:])
+                nc.tensor.transpose(ps_bb[:, m, :], xbT[:, 3, m : m + 1].to_broadcast([P, P]), ident_b[:])
             nc.scalar.copy(out=bias_bc[:], in_=ps_bb[:].rearrange("p m n -> p (m n)"))
-            wlT = keep.tile([P, 3, N], BF16, name="wlT")
-            for j in range(3):
-                ps_w = ps_tp.tile([P, 3, P], BF16, name="ps_w", tag="tp")
+
+        def deep_turn_w(j_lo, j_hi):
+            ps_w = ps_tp.tile([P, j_hi - j_lo, 3, P], BF16, name="ps_w", tag="tp")
+            for j in range(j_lo, j_hi):
                 for a in range(3):
-                    nc.tensor.transpose(ps_w[:, a, :], wl_sb[:, a, P * j : P * j + P], ident_b[:])
-                nc.scalar.copy(out=wlT[:, j, :], in_=ps_w[:].rearrange("p a n -> p (a n)"))
+                    nc.tensor.transpose(ps_w[:, j - j_lo, a, :], wl_sb[:, a, P * j : P * j + P], ident_b[:])
+            nc.scalar.copy(out=wlT[:, j_lo:j_hi, :], in_=ps_w[:].rearrange("p j a n -> p j (a n)"))
+
+        def deep_multiply():
             acc_g = ps_tp.tile([P, N], F32, name="acc_g", tag="tp")
             for j in range(3):
-                nc.tensor.matmul(acc_g[:], lhsT=xT[:, j, :], rhs=wlT[:, j, :], start=(j == 0), stop=(j == 2))
-            return acc_g
+                nc.tensor.matmul(acc_g[:], lhsT=xbT[:, j, :], rhs=wlT[:, j, :], start=(j == 0), stop=(j == 2))
+            late["acc_g"] = acc_g
+
+        deep_stage = {
+            5: deep_turn_x,
+            7: deep_spread_bias,
+            9: lambda: deep_turn_w(0, 2),
+            11: lambda: deep_turn_w(2, 3),
+            13: deep_multiply,
+        }
 
         for step in range(BANKS + LEAD):
+            if step < PERIOD:
+                turn_ht(step)
             if step < BANKS:
                 spread(step)
-                if step % 3 == 0 and step // 3 + 1 < 4:
-                    build_sel(step // 3 + 1)
+            if step in deep_stage:
+                deep_stage[step]()
             if 0 <= step - 1 < BANKS:
                 product(step - 1)
+            if step < PERIOD:
+                keep_ht(step)
             if 0 <= step - 2 < BANKS:
                 quantise(step - 2)
             if 0 <= step - LEAD < BANKS:
                 passes(step - LEAD)
-            if step == 8:
-                acc_g = deep()
             if step == BANKS + 2:
                 g_sb = keep.tile([P, N], F32, name="g_sb")
-                nc.vector.tensor_tensor(out=g_sb[:], in0=acc_g[:], in1=bias_bc[:, 0:N], op=ADD)
+                nc.vector.tensor_tensor(out=g_sb[:], in0=late["acc_g"][:], in1=bias_bc[:, 0:N], op=ADD)
                 nc.sync.dma_start(out=out[:, 0:N], in_=g_sb[:])
 
         u_sb = keep.tile([P, N], F32, name="u_sb")

@@ -23,7 +23,7 @@ WPI = D // 4
 PERIOD = 3
 GPB = 4
 BANKS = GROUPS // GPB
-LEAD = 3
+LEAD = 10
 
 FLOPS = 2 * B * D * D * N + 2 * B * N * N
 
@@ -58,12 +58,12 @@ def tile_deepandwide_w_kernel(tc, hspatial, htext, W_L, b_L, W_L2_words, W_L2_sc
         nc.sync.dma_start(out=x_sb[:, D : 2 * D], in_=htext)
         nc.scalar.dma_start(out=bt[0:3, :], in_=b_L.rearrange("(a n) -> a n", a=3))
         nc.scalar.dma_start(out=bt[3:6, :], in_=b_L2.rearrange("(a n) -> a n", a=3))
-        sc_view = W_L2_scales.bitcast(I32).rearrange("(col a) q w -> q a col w", a=4)
+        sc_view = W_L2_scales.bitcast(F32).rearrange("(col a) q w -> q a col w", a=4)
         for quad in range(4):
             for r in range(4):
-                nc.sync.dma_start(
+                nc.gpsimd.dma_start(
                     out=planes[32 * quad + r : 32 * quad + 16 : 4, :]
-                    .bitcast(I32)
+                    .bitcast(F32)
                     .rearrange("a (col w) -> a col w", w=N // 4),
                     in_=sc_view[4 * quad + r],
                 )

@@ -24,6 +24,7 @@ PERIOD = 3
 GPB = 4
 BANKS = GROUPS // GPB
 LEAD = 10
+ON_SYNC = 6
 
 FLOPS = 2 * B * D * D * N + 2 * B * N * N
 
@@ -58,15 +59,15 @@ def tile_deepandwide_w_kernel(tc, hspatial, htext, W_L, b_L, W_L2_words, W_L2_sc
         nc.sync.dma_start(out=x_sb[:, D : 2 * D], in_=htext)
         nc.scalar.dma_start(out=bt[0:3, :], in_=b_L.rearrange("(a n) -> a n", a=3))
         nc.scalar.dma_start(out=bt[3:6, :], in_=b_L2.rearrange("(a n) -> a n", a=3))
-        sc_view = W_L2_scales.bitcast(F32).rearrange("(col a) q w -> q a col w", a=4)
-        for quad in range(4):
-            for r in range(4):
-                nc.gpsimd.dma_start(
-                    out=planes[32 * quad + r : 32 * quad + 16 : 4, :]
-                    .bitcast(F32)
-                    .rearrange("a (col w) -> a col w", w=N // 4),
-                    in_=sc_view[4 * quad + r],
-                )
+        for q in range(16):
+            quad, r = divmod(q, 4)
+            queue, word = (nc.sync, I32) if q < ON_SYNC else (nc.gpsimd, F32)
+            queue.dma_start(
+                out=planes[32 * quad + r : 32 * quad + 16 : 4, :]
+                .bitcast(word)
+                .rearrange("a (col w) -> a col w", w=N // 4),
+                in_=W_L2_scales.bitcast(word).rearrange("(col a) q w -> q a col w", a=4)[q],
+            )
         w_view = (
             W_L2_words.rearrange("g p n t -> g p (n t)")
             .bitcast(I32)

@@ -25,6 +25,7 @@ GPB = 4
 BANKS = GROUPS // GPB
 LEAD = 10
 ON_SYNC = 6
+WIDE_SUPS = 5
 
 FLOPS = 2 * B * D * D * N + 2 * B * N * N
 
@@ -45,7 +46,8 @@ def tile_deepandwide_w_kernel(tc, hspatial, htext, W_L, b_L, W_L2_words, W_L2_sc
         ident_b = keep.tile([P, P], BF16, name="ident_b")
         ident_f = keep.tile([P, P], F32, name="ident_f")
         wl_sb = keep.tile([P, 3, N], BF16, name="wl_sb")
-        w_tiles = [keep.tile([P, GPB, 4 * N], U8, name="w%d" % n, align_bytes=64) for n in range(BANKS)]
+        w_sup = [keep.tile([P, PERIOD * GPB, 4 * N], U8, name="ws%d" % s, align_bytes=64) for s in range(WIDE_SUPS)]
+        w_tiles = {n: keep.tile([P, GPB, 4 * N], U8, name="w%d" % n, align_bytes=64) for n in range(PERIOD * WIDE_SUPS, BANKS)}
         vw = [keep.tile([P, GPB * B], U32, name="vw%d" % n, align_bytes=64) for n in range(BANKS)]
         vpl = [keep.tile([P, GPB * B], U8, name="vpl%d" % n, align_bytes=64) for n in range(BANKS)]
         hrep = [keep.tile([P, 32, WPI], F32, name="hrep%d" % s) for s in range(6)]
@@ -73,15 +75,18 @@ def tile_deepandwide_w_kernel(tc, hspatial, htext, W_L, b_L, W_L2_words, W_L2_sc
             .bitcast(I32)
             .rearrange("(G c) p w -> c p G w", c=PERIOD)
         )
-        for n in range(BANKS):
+        w_flat = W_L2_words.rearrange("g p n t -> g p (n t)").bitcast(I32).rearrange("g p w -> p g w")
+        for s in range(WIDE_SUPS):
+            nc.sync.dma_start(out=w_sup[s][:].bitcast(I32), in_=w_flat[:, 12 * s : 12 * s + 12, :])
+            if s == 0:
+                nc.sync.dma_start(out=wl_sb[:], in_=W_L.rearrange("(a p) k -> p a k", p=P))
+        for n in range(PERIOD * WIDE_SUPS, BANKS):
             sup, c = divmod(n, PERIOD)
             src = w_view[c]
             dst = w_tiles[n][:].bitcast(I32)
             cuts = [(0, 4)] if n < BANKS - 1 else [(0, 2), (2, 3), (3, 4)]
             for lo, hi in cuts:
                 nc.sync.dma_start(out=dst[:, lo:hi, :], in_=src[:, GPB * sup + lo : GPB * sup + hi, :])
-            if n == 1:
-                nc.sync.dma_start(out=wl_sb[:], in_=W_L.rearrange("(a p) k -> p a k", p=P))
 
         hsp = keep.tile([P, D, 2], BF16, name="hsp")
         nc.vector.tensor_copy(out=hsp[:], in_=x_sb[:, 0:D].unsqueeze(2).to_broadcast([P, D, 2]))
@@ -172,7 +177,9 @@ def tile_deepandwide_w_kernel(tc, hspatial, htext, W_L, b_L, W_L2_words, W_L2_sc
             )
 
         def passes(n):
+            sup, c = divmod(n, PERIOD)
             for gi in range(GPB):
+                words = w_sup[sup][:, PERIOD * gi + c, :] if sup < WIDE_SUPS else w_tiles[n][:, gi, :]
                 g = group_of(n, gi)
                 col, a = divmod(g, 4)
                 first = n == 0 and gi == 0
@@ -182,7 +189,7 @@ def tile_deepandwide_w_kernel(tc, hspatial, htext, W_L, b_L, W_L2_words, W_L2_sc
                         out=acc[:],
                         lhsT=vw[n][:, B * gi : B * gi + B].bitcast(FP8X4),
                         lhsT_scale=vpl[n][:, B * gi : B * gi + B],
-                        rhs=w_tiles[n][:, gi, 4 * lo : 4 * hi].bitcast(FP8X4),
+                        rhs=words[:, 4 * lo : 4 * hi].bitcast(FP8X4),
                         rhs_scale=planes[4 * a : P, N * col + lo : N * col + hi],
                         start=first,
                         stop=last,

@@ -59,8 +59,13 @@ def tile_deepandwide_w_kernel(tc, hspatial, htext, W_L, b_L, W_L2_words, W_L2_sc
 
         nc.sync.dma_start(out=x_sb[:, 0:D], in_=hspatial)
         nc.sync.dma_start(out=x_sb[:, D : 2 * D], in_=htext)
-        nc.scalar.dma_start(out=bt[0:3, :], in_=b_L.rearrange("(a n) -> a n", a=3))
-        nc.scalar.dma_start(out=bt[3:6, :], in_=b_L2.rearrange("(a n) -> a n", a=3))
+        w_flat = W_L2_words.rearrange("g p n t -> g p (n t)").bitcast(I32).rearrange("g p w -> p g w")
+
+        def load_sup(s):
+            nc.sync.dma_start(out=w_sup[s][:].bitcast(I32), in_=w_flat[:, 12 * s : 12 * s + 12, :])
+
+        nc.sync.dma_start(out=wl_sb[:], in_=W_L.rearrange("(a p) k -> p a k", p=P))
+        load_sup(0)
         for q in range(16):
             quad, r = divmod(q, 4)
             queue, word = (nc.sync, I32) if q < ON_SYNC else (nc.gpsimd, F32)
@@ -75,11 +80,10 @@ def tile_deepandwide_w_kernel(tc, hspatial, htext, W_L, b_L, W_L2_words, W_L2_sc
             .bitcast(I32)
             .rearrange("(G c) p w -> c p G w", c=PERIOD)
         )
-        w_flat = W_L2_words.rearrange("g p n t -> g p (n t)").bitcast(I32).rearrange("g p w -> p g w")
-        for s in range(WIDE_SUPS):
-            nc.sync.dma_start(out=w_sup[s][:].bitcast(I32), in_=w_flat[:, 12 * s : 12 * s + 12, :])
-            if s == 0:
-                nc.sync.dma_start(out=wl_sb[:], in_=W_L.rearrange("(a p) k -> p a k", p=P))
+        nc.gpsimd.dma_start(out=bt[0:3, :], in_=b_L.rearrange("(a n) -> a n", a=3))
+        nc.gpsimd.dma_start(out=bt[3:6, :], in_=b_L2.rearrange("(a n) -> a n", a=3))
+        for s in range(1, WIDE_SUPS):
+            load_sup(s)
         for n in range(PERIOD * WIDE_SUPS, BANKS):
             sup, c = divmod(n, PERIOD)
             src = w_view[c]
@@ -228,11 +232,11 @@ def tile_deepandwide_w_kernel(tc, hspatial, htext, W_L, b_L, W_L2_words, W_L2_sc
             late["acc_g"] = acc_g
 
         deep_stage = {
-            5: deep_turn_x,
-            7: deep_spread_bias,
-            9: lambda: deep_turn_w(0, 2),
-            11: lambda: deep_turn_w(2, 3),
-            13: deep_multiply,
+            7: lambda: deep_turn_w(0, 2),
+            9: lambda: deep_turn_w(2, 3),
+            13: deep_turn_x,
+            15: deep_spread_bias,
+            16: deep_multiply,
         }
 
         for step in range(BANKS + LEAD):

@@ -114,8 +114,6 @@ def tile_deepandwide_w_kernel(tc, hspatial, htext, W_L, b_L, W_L2_words, W_L2_sc
             .to_broadcast([P, 2, 8, WPI]),
         )
         build_hrep(nc.vector.tensor_copy, 0, 16, 32)
-        for s in range(1, 6):
-            build_hrep(nc.scalar.copy, s, 0, 32)
         htx_flat = htx[:].rearrange("p u a r -> p u (a r)")
         ht = []
 
@@ -129,7 +127,8 @@ def tile_deepandwide_w_kernel(tc, hspatial, htext, W_L, b_L, W_L2_words, W_L2_sc
 
         def keep_ht(c):
             ht_c = keep.tile([P, B, 2, 2], BF16, name="ht%d" % c)
-            nc.vector.tensor_copy(
+            copy = nc.vector.tensor_copy if c == 0 else nc.scalar.copy
+            copy(
                 out=ht_c[:].rearrange("p b u e -> p (b u e)").bitcast(F32).rearrange("p (b u) -> p b u", u=2),
                 in_=pht_of[c][:].rearrange("p u b -> p b u"),
             )
@@ -250,6 +249,8 @@ def tile_deepandwide_w_kernel(tc, hspatial, htext, W_L, b_L, W_L2_words, W_L2_sc
                 product(step - 1)
             if step < PERIOD:
                 keep_ht(step)
+            if 2 <= step <= 6:
+                build_hrep(nc.scalar.copy, step - 1, 0, 32)
             if 0 <= step - 2 < BANKS:
                 quantise(step - 2)
             if 0 <= step - LEAD < BANKS:

from contextlib import ExitStack

import concourse.bass as bass
import concourse.mybir as mybir
import concourse.tile as tile
from concourse.masks import make_identity

BF16 = mybir.dt.bfloat16
F32 = mybir.dt.float32
I32 = mybir.dt.int32
U8 = mybir.dt.uint8
U32 = mybir.dt.uint32
FP8X4 = mybir.dt.float8_e4m3fn_x4
MULT = mybir.AluOpType.mult
ADD = mybir.AluOpType.add

P = 128
B = 128
D = 192
N = 2 * D
GROUPS = D * D // 512
WPI = D // 4
PERIOD = 3
GPB = 4
BANKS = GROUPS // GPB
LEAD = 10
ON_SYNC = 6
WIDE_SUPS = 5

FLOPS = 2 * B * D * D * N + 2 * B * N * N


def tile_deepandwide_w_kernel(tc, hspatial, htext, W_L, b_L, W_L2_words, W_L2_scales, b_L2, out):
    nc = tc.nc
    with ExitStack() as ctx:
        keep = ctx.enter_context(tc.tile_pool(name="keep", bufs=1))
        ring = ctx.enter_context(tc.tile_pool(name="ring", bufs=3))
        ps_acc = ctx.enter_context(tc.psum_pool(name="ps_acc", bufs=1))
        ps_hs = ctx.enter_context(tc.psum_pool(name="ps_hs", bufs=4))
        ps_tp = ctx.enter_context(tc.psum_pool(name="ps_tp", bufs=2))
        ctx.enter_context(tc.manual_schedule())

        x_sb = keep.tile([P, 2 * D], BF16, name="x_sb", align_bytes=64)
        bt = keep.tile([P, P], BF16, name="bt")
        planes = keep.tile([P, (GROUPS // 4) * N], U8, name="planes", align_bytes=64)
        ident_b = keep.tile([P, P], BF16, name="ident_b")
        ident_f = keep.tile([P, P], F32, name="ident_f")
        wl_sb = keep.tile([P, 3, N], BF16, name="wl_sb")
        w_sup = [keep.tile([P, PERIOD * GPB, 4 * N], U8, name="ws%d" % s, align_bytes=64) for s in range(WIDE_SUPS)]
        w_tiles = {n: keep.tile([P, GPB, 4 * N], U8, name="w%d" % n, align_bytes=64) for n in range(PERIOD * WIDE_SUPS, BANKS)}
        vw = [keep.tile([P, GPB * B], U32, name="vw%d" % n, align_bytes=64) for n in range(BANKS)]
        vpl = [keep.tile([P, GPB * B], U8, name="vpl%d" % n, align_bytes=64) for n in range(BANKS)]
        hrep = [keep.tile([P, 32, WPI], F32, name="hrep%d" % s) for s in range(6)]

        nc.vector.memset(bt[:], 0.0)
        nc.vector.memset(planes[:].bitcast(I32), 0)
        make_identity(nc, ident_f[:])
        make_identity(nc, ident_b[:])

        nc.sync.dma_start(out=x_sb[:, 0:D], in_=hspatial)
        nc.sync.dma_start(out=x_sb[:, D : 2 * D], in_=htext)
        w_flat = W_L2_words.rearrange("g p n t -> g p (n t)").bitcast(I32).rearrange("g p w -> p g w")

        def load_sup(s):
            nc.sync.dma_start(out=w_sup[s][:].bitcast(I32), in_=w_flat[:, 12 * s : 12 * s + 12, :])

        nc.sync.dma_start(out=wl_sb[:], in_=W_L.rearrange("(a p) k -> p a k", p=P))
        load_sup(0)
        for q in range(16):
            quad, r = divmod(q, 4)
            queue, word = (nc.sync, I32) if q < ON_SYNC else (nc.gpsimd, F32)
            queue.dma_start(
                out=planes[32 * quad + r : 32 * quad + 16 : 4, :]
                .bitcast(word)
                .rearrange("a (col w) -> a col w", w=N // 4),
                in_=W_L2_scales.bitcast(word).rearrange("(col a) q w -> q a col w", a=4)[q],
            )
        w_view = (
            W_L2_words.rearrange("g p n t -> g p (n t)")
            .bitcast(I32)
            .rearrange("(G c) p w -> c p G w", c=PERIOD)
        )
        nc.gpsimd.dma_start(out=bt[0:3, :], in_=b_L.rearrange("(a n) -> a n", a=3))
        nc.gpsimd.dma_start(out=bt[3:6, :], in_=b_L2.rearrange("(a n) -> a n", a=3))
        for s in range(1, WIDE_SUPS):
            load_sup(s)
        for n in range(PERIOD * WIDE_SUPS, BANKS):
            sup, c = divmod(n, PERIOD)
            src = w_view[c]
            dst = w_tiles[n][:].bitcast(I32)
            cuts = [(0, 4)] if n < BANKS - 1 else [(0, 2), (2, 3), (3, 4)]
            for lo, hi in cuts:
                nc.sync.dma_start(out=dst[:, lo:hi, :], in_=src[:, GPB * sup + lo : GPB * sup + hi, :])

        hsp = keep.tile([P, D, 2], BF16, name="hsp")
        nc.vector.tensor_copy(out=hsp[:], in_=x_sb[:, 0:D].unsqueeze(2).to_broadcast([P, D, 2]))
        hsp_w = hsp[:].rearrange("p i e -> p (i e)").bitcast(F32)

        def build_hrep(eng_copy, s, lo, hi):
            eng_copy(
                out=hrep[s][:, lo:hi, :],
                in_=hsp_w[:, 32 * s + lo : 32 * s + hi].unsqueeze(2).to_broadcast([P, hi - lo, WPI]),
            )

        build_hrep(nc.scalar.copy, 0, 0, 16)

        htx = keep.tile([P, 2, 8, WPI], F32, name="htx")
        nc.vector.tensor_copy(
            out=htx[:],
            in_=x_sb[:, D : 2 * D]
            .bitcast(F32)
            .rearrange("p (r u) -> p u r", u=2)
            .unsqueeze(2)
            .to_broadcast([P, 2, 8, WPI]),
        )
        build_hrep(nc.vector.tensor_copy, 0, 16, 32)
        htx_flat = htx[:].rearrange("p u a r -> p u (a r)")
        ht = []

        pht_of = {}

        def turn_ht(c):
            pht = ps_tp.tile([P, 2, P], F32, name="pht%d" % c, tag="tp")
            for u in range(2):
                nc.tensor.transpose(pht[:, u, :], htx_flat[:, u, P * c : P * c + P], ident_f[:])
            pht_of[c] = pht

        def keep_ht(c):
            ht_c = keep.tile([P, B, 2, 2], BF16, name="ht%d" % c)
            copy = nc.vector.tensor_copy if c == 0 else nc.scalar.copy
            copy(
                out=ht_c[:].rearrange("p b u e -> p (b u e)").bitcast(F32).rearrange("p (b u) -> p b u", u=2),
                in_=pht_of[c][:].rearrange("p u b -> p b u"),
            )
            ht.append(ht_c)

        acc_a = ps_acc.tile([P, 256], F32, name="acc_a")
        acc_b = ps_acc.tile([P, 128], F32, name="acc_b")

        hs2_of = {}
        vin_of = {}

        def group_of(n, gi):
            sup, c = divmod(n, PERIOD)
            return PERIOD * (GPB * sup + gi) + c

        def spread(n):
            sup, c = divmod(n, PERIOD)
            hs_ps = ps_hs.tile([P, GPB, B], F32, name="hs_ps", tag="hs")
            for gi in range(GPB):
                blk = PERIOD * gi + c
                nc.tensor.transpose(
                    hs_ps[:, gi, :],
                    hrep[sup][:].rearrange("p i r -> p (i r)")[:, P * blk : P * blk + P],
                    ident_f[:],
                )
            hs2_of[n] = hs_ps

        def product(n):
            c = n % PERIOD
            vin = ring.tile([P, GPB, B, 2, 2], BF16, name="vin", tag="vin", align_bytes=64)
            nc.vector.tensor_tensor(
                out=vin[:],
                in0=ht[c][:].unsqueeze(1).to_broadcast([P, GPB, B, 2, 2]),
                in1=hs2_of[n][:]
                .rearrange("p g b -> p (g b)")
                .bitcast(BF16)
                .rearrange("p (g b e) -> p g b e", g=GPB, e=2)
                .unsqueeze(3)
                .to_broadcast([P, GPB, B, 2, 2]),
                op=MULT,
            )
            vin_of[n] = vin

        def quantise(n):
            nc.vector.quantize_mx(
                out=vw[n][:].bitcast(FP8X4),
                scales=vpl[n][:],
                in_=vin_of[n][:].rearrange("p g b u e -> p (g b u e)"),
            )

        def passes(n):
            sup, c = divmod(n, PERIOD)
            for gi in range(GPB):
                words = w_sup[sup][:, PERIOD * gi + c, :] if sup < WIDE_SUPS else w_tiles[n][:, gi, :]
                g = group_of(n, gi)
                col, a = divmod(g, 4)
                first = n == 0 and gi == 0
                last = n == BANKS - 1 and gi == GPB - 1
                for acc, lo, hi in ((acc_a, 0, 256), (acc_b, 256, 384)):
                    nc.tensor.matmul_mx(
                        out=acc[:],
                        lhsT=vw[n][:, B * gi : B * gi + B].bitcast(FP8X4),
                        lhsT_scale=vpl[n][:, B * gi : B * gi + B],
                        rhs=words[:, 4 * lo : 4 * hi].bitcast(FP8X4),
                        rhs_scale=planes[4 * a : P, N * col + lo : N * col + hi],
                        start=first,
                        stop=last,
                    )

        bias_bc = keep.tile([P, 2 * N], F32, name="bias_bc")

        xbT = keep.tile([P, 4, P], BF16, name="xbT")
        wlT = keep.tile([P, 3, N], BF16, name="wlT")
        late = {}

        def deep_turn_x():
            ps_x = ps_tp.tile([P, 4, P], BF16, name="ps_x", tag="tp")
            for j in range(3):
                nc.tensor.transpose(ps_x[:, j, :], x_sb[:, P * j : P * j + P], ident_b[:])
            nc.tensor.transpose(ps_x[:, 3, :], bt[:], ident_b[:])
            nc.scalar.copy(out=xbT[:], in_=ps_x[:])

        def deep_spread_bias():
            ps_bb = ps_tp.tile([P, 6, P], BF16, name="ps_bb", tag="tp")
            for m in range(6):
                nc.tensor.transpose(ps_bb[:, m, :], xbT[:, 3, m : m + 1].to_broadcast([P, P]), ident_b[:])
            nc.scalar.copy(out=bias_bc[:], in_=ps_bb[:].rearrange("p m n -> p (m n)"))

        def deep_turn_w(j_lo, j_hi):
            ps_w = ps_tp.tile([P, j_hi - j_lo, 3, P], BF16, name="ps_w", tag="tp")
            for j in range(j_lo, j_hi):
                for a in range(3):
                    nc.tensor.transpose(ps_w[:, j - j_lo, a, :], wl_sb[:, a, P * j : P * j + P], ident_b[:])
            nc.scalar.copy(out=wlT[:, j_lo:j_hi, :], in_=ps_w[:].rearrange("p j a n -> p j (a n)"))

        def deep_multiply():
            acc_g = ps_tp.tile([P, N], F32, name="acc_g", tag="tp")
            for j in range(3):
                nc.tensor.matmul(acc_g[:], lhsT=xbT[:, j, :], rhs=wlT[:, j, :], start=(j == 0), stop=(j == 2))
            late["acc_g"] = acc_g

        deep_stage = {
            7: lambda: deep_turn_w(0, 2),
            9: lambda: deep_turn_w(2, 3),
            13: deep_turn_x,
            15: deep_spread_bias,
            16: deep_multiply,
        }

        for step in range(BANKS + LEAD):
            if step < PERIOD:
                turn_ht(step)
            if step < BANKS:
                spread(step)
            if step in deep_stage:
                deep_stage[step]()
            if 0 <= step - 1 < BANKS:
                product(step - 1)
            if step < PERIOD:
                keep_ht(step)
            if 2 <= step <= 6:
                build_hrep(nc.scalar.copy, step - 1, 0, 32)
            if 0 <= step - 2 < BANKS:
                quantise(step - 2)
            if 0 <= step - LEAD < BANKS:
                passes(step - LEAD)
            if step == BANKS + 2:
                g_sb = keep.tile([P, N], F32, name="g_sb")
                nc.vector.tensor_tensor(out=g_sb[:], in0=late["acc_g"][:], in1=bias_bc[:, 0:N], op=ADD)
                nc.sync.dma_start(out=out[:, 0:N], in_=g_sb[:])

        u_sb = keep.tile([P, N], F32, name="u_sb")
        nc.vector.tensor_tensor(out=u_sb[:, 0:256], in0=acc_a[:], in1=bias_bc[:, N : N + 256], op=ADD)
        nc.vector.tensor_tensor(out=u_sb[:, 256:N], in0=acc_b[:], in1=bias_bc[:, N + 256 : 2 * N], op=ADD)
        nc.sync.dma_start(out=out[:, N : 2 * N], in_=u_sb[:])
